import numpy as np
import ml_dtypes


def mxq(x, axis, fmt="e4m3"):
    dtype, down = {"e4m3": (ml_dtypes.float8_e4m3fn, 7), "e5m2": (ml_dtypes.float8_e5m2, 14)}[fmt]
    v = np.moveaxis(np.asarray(x, np.float32).astype(ml_dtypes.bfloat16).astype(np.float64), axis, -1)
    blocks = v.reshape(v.shape[:-1] + (-1, 32))
    amax = np.abs(blocks).max(-1, keepdims=True)
    byte = np.maximum(np.where(amax > 0, np.frexp(amax)[1] - 1 + 127, 0) - down, 1)
    scale = np.exp2(byte - 127.0)
    codes = (blocks / scale).astype(np.float32).astype(dtype).astype(np.float64)
    return np.moveaxis((codes * scale).reshape(v.shape), -1, axis)


WIDE = False


def mx_kscale(k):
    if not WIDE:
        return np.ones(k)
    levels = np.array([10, -10, 5, -5, 0])
    if k % 512:
        return np.exp2(np.random.permutation(np.resize(levels, k // 32))).repeat(32)
    a = np.empty((k // 512, 16))
    for p in range(k // 512):
        a[p, :8] = np.random.permutation(np.resize(levels, 8))
        for g in range(8):
            far = levels[np.abs(levels - a[p, g]) >= 10]
            a[p, g + 8] = far[np.random.randint(len(far))]
    return np.exp2(a.ravel()).repeat(32)


BF16 = ml_dtypes.bfloat16


def bf(x):
    return np.asarray(x, np.float32).astype(BF16)


def f64(x):
    return np.asarray(x).astype(np.float64)


B, IN, L = 4096, 1024, 256


def sigmoid(v):
    return 1.0 / (1.0 + np.exp(-v))


def setup_inputs():
    s = mx_kscale(IN)
    return {"input": bf(np.random.standard_normal((B, IN)) * s),
            "h0": bf(np.random.standard_normal((B, L))),
            "gh0": bf(np.random.standard_normal((B, 3 * L)) * 0.75),
            "W_ih0": bf(np.random.standard_normal((3 * L, IN)) * 0.7 / np.sqrt(IN) / s),
            "b_ih0": bf(np.random.standard_normal(3 * L) * 0.3)}


def reference(input, h0, gh0, W_ih0, b_ih0):
    h, gh = f64(h0), f64(gh0)
    gi = (mxq(f64(input), 1, "e4m3") @ mxq(f64(W_ih0), 1, "e4m3").T) + f64(b_ih0)
    i_r, i_z, i_n = gi[:, :L], gi[:, L:2 * L], gi[:, 2 * L:]
    h_r, h_z, h_n = gh[:, :L], gh[:, L:2 * L], gh[:, 2 * L:]
    r = sigmoid(i_r + h_r)
    z = sigmoid(i_z + h_z)
    n = np.tanh(i_n + r * h_n)
    return (1.0 - z) * n + z * h

@@ -1,0 +1,299 @@
+from contextlib import ExitStack
+
+import concourse.mybir as mybir
+from concourse.masks import make_identity
+
+F32 = mybir.dt.float32
+BF16 = mybir.dt.bfloat16
+U32 = mybir.dt.uint32
+U8 = mybir.dt.uint8
+FP8X4 = mybir.dt.float8_e4m3fn_x4
+ACT = mybir.ActivationFunctionType
+ALU = mybir.AluOpType
+
+P = 128
+B = 4096
+IN = 1024
+L = 256
+G3 = 3 * L
+NT = B // P
+GRP = 4
+NG = NT // GRP
+WT = G3 // P
+PIN = True
+
+FLOPS = 2 * B * IN * G3
+
+
+def tile_grucellstack_pa_t_kernel(tc, x, h0, gh0, w_ih0, b_ih0, out):
+    nc = tc.nc
+    x_v = x.rearrange("(p t) k -> p (t k)", t=NT)
+    g_v = gh0.rearrange("(p t) c -> p t c", t=NT)
+    h_v = h0.rearrange("(p t) c -> p t c", t=NT)
+    o_v = out.rearrange("(p t) c -> p t c", t=NT)
+    w_v = w_ih0.rearrange("(t p) k -> p t k", p=P)
+    n = GRP * P
+
+    with ExitStack() as ctx:
+        if PIN:
+            ctx.enter_context(tc.manual_schedule())
+        const = ctx.enter_context(tc.tile_pool(name="const", bufs=1))
+        xin = ctx.enter_context(tc.tile_pool(name="xin", bufs=4))
+        gin = ctx.enter_context(tc.tile_pool(name="gin", bufs=NG))
+        hin = ctx.enter_context(tc.tile_pool(name="hin", bufs=NG))
+        grp = ctx.enter_context(tc.tile_pool(name="grp", bufs=2))
+        cod = ctx.enter_context(tc.tile_pool(name="cod", bufs=3))
+        pbp = ctx.enter_context(tc.tile_pool(name="pbp", bufs=2))
+        rzp = ctx.enter_context(tc.tile_pool(name="rzp", bufs=3))
+        vpl = ctx.enter_context(tc.tile_pool(name="vpl", bufs=4))
+        upl = ctx.enter_context(tc.tile_pool(name="upl", bufs=2))
+        opl = ctx.enter_context(tc.tile_pool(name="opl", bufs=3))
+        psum = ctx.enter_context(tc.psum_pool(name="psum", bufs=8))
+
+        brow = const.tile([P, P], BF16)
+        nc.vector.memset(brow[:], 0.0)
+        bz = const.tile([P, L], BF16)
+        nc.vector.memset(bz[:], 0.0)
+        ones = const.tile([P, P], BF16)
+        nc.vector.memset(ones[:], 1.0)
+        ident = const.tile([P, P], F32)
+        make_identity(nc, ident[:])
+        identb = const.tile([P, P], BF16)
+        make_identity(nc, identb[:])
+
+        x_sb = {}
+        g_sb = {}
+        h_sb = {}
+        w_sb = const.tile([P, WT, IN], BF16)
+
+        def load_x(c, pieces):
+            xt_in = xin.tile([P, GRP * IN], BF16)
+            w = GRP * IN // pieces
+            for k in range(pieces):
+                nc.sync.dma_start(out=xt_in[:, k * w:(k + 1) * w], in_=x_v[:, c * GRP * IN + k * w:c * GRP * IN + (k + 1) * w])
+            x_sb[c] = xt_in
+
+        def load_gh(c):
+            gt_in = gin.tile([P, GRP, G3], BF16)
+            nc.sync.dma_start(out=gt_in[:], in_=g_v[:, c * GRP:(c + 1) * GRP, :])
+            g_sb[c] = gt_in
+            ht_in = hin.tile([P, GRP, L], BF16)
+            nc.sync.dma_start(out=ht_in[:], in_=h_v[:, c * GRP:(c + 1) * GRP, :])
+            h_sb[c] = ht_in
+
+        nc.sync.dma_start(out=brow[0:WT, :], in_=b_ih0.rearrange("(r c) -> r c", c=P))
+        nc.sync.dma_start(out=bz[0:1, :], in_=b_ih0.rearrange("(o c) -> o c", o=1)[:, 2 * L:G3])
+        load_x(0, 4)
+        for i in range(3):
+            nc.sync.dma_start(out=w_sb[:, 2 * i:2 * i + 2, :], in_=w_v[:, 2 * i:2 * i + 2, :])
+        load_x(1, 1)
+        load_gh(0)
+        load_x(2, 1)
+        load_gh(1)
+        load_x(3, 1)
+
+        bt_ps = psum.tile([P, P], BF16, tag="bank")
+        nc.tensor.transpose(bt_ps[:], brow[:], identb[:])
+        bias_col = const.tile([P, 8], F32)
+        nc.vector.tensor_copy(out=bias_col[:, 0:WT], in_=bt_ps[:, 0:WT])
+        bn_ps = psum.tile([P, L], F32, tag="bank")
+        nc.tensor.matmul(out=bn_ps[:], lhsT=ones[:], rhs=bz[:], start=True, stop=True)
+        bn_sb = const.tile([P, L], F32)
+        nc.vector.tensor_copy(out=bn_sb[:], in_=bn_ps[:])
+
+        wcodes = const.tile([P, 2 * G3], U32, align_bytes=64)
+        wscl = const.tile([P, 2 * G3], U8, align_bytes=64)
+
+        def turn(words, col0, dst, on_vector):
+            xt = psum.tile([P, 4, P], F32, tag="bank")
+            for q in range(4):
+                w0 = col0 + (q // 2) * 2 * P + q % 2
+                nc.tensor.transpose(xt[:, q, :], words[:, w0:w0 + 2 * P - 1:2], ident[:])
+            src = xt[:].rearrange("p (g u) r -> p g r u", u=2)
+            if on_vector:
+                nc.vector.tensor_copy(out=dst, in_=src)
+            else:
+                nc.scalar.copy(out=dst, in_=src)
+
+        groupeds = {}
+        xc = {}
+        pbts = {}
+        pns = {}
+        vs = {}
+        us = {}
+        rzs = {}
+        outs = {}
+
+        def a_begin(c):
+            grouped = grp.tile([P, 8 * n], BF16, align_bytes=64)
+            groupeds[c] = grouped
+
+        def a_tile(c, j, on_vector):
+            gw = groupeds[c][:].bitcast(F32).rearrange("p (g r u) -> p g r u", g=2, u=2)
+            turn(x_sb[c][:].bitcast(F32), j * (IN // 2), gw[:, :, j * P:(j + 1) * P, :], on_vector)
+
+        def a_end(c):
+            codes = cod.tile([P, 2 * n], U32, align_bytes=64)
+            scl = cod.tile([P, 2 * n], U8, align_bytes=64)
+            nc.vector.quantize_mx(out=codes[:].bitcast(FP8X4), scales=scl[:], in_=groupeds[c][:])
+            xc[c] = (codes, scl)
+
+        def prep_w():
+            for half in range(3):
+                wg = grp.tile([P, 8 * n], BF16, align_bytes=64, tag="grouped")
+                for k in range(2):
+                    lt = 2 * half + k
+                    dst = wg[:, k * 8 * P:(k + 1) * 8 * P].bitcast(F32).rearrange("p (g r u) -> p g r u", g=2, u=2)
+                    turn(w_sb[:, lt, :].bitcast(F32), 0, dst, k == 1)
+                for k in range(2):
+                    lt = 2 * half + k
+                    for g in range(2):
+                        c0 = g * G3 + lt * P
+                        nc.vector.quantize_mx(
+                            out=wcodes[:, c0:c0 + P].bitcast(FP8X4),
+                            scales=wscl[:, c0:c0 + P],
+                            in_=wg[:, (2 * k + g) * 4 * P:(2 * k + g + 1) * 4 * P],
+                        )
+
+        def b_rz(c, share_with_vector):
+            codes, scl = xc[c]
+            pbt = pbp.tile([P, 4, n], F32)
+            pbts[c] = pbt
+            for lt in range(4):
+                pt = psum.tile([P, n], F32, tag="bank")
+                for g in range(2):
+                    c0 = g * G3 + lt * P
+                    nc.tensor.matmul_mx(
+                        out=pt[:],
+                        lhsT=wcodes[:, c0:c0 + P].bitcast(FP8X4), lhsT_scale=wscl[:, c0:c0 + P],
+                        rhs=codes[:, g * n:(g + 1) * n].bitcast(FP8X4), rhs_scale=scl[:, g * n:(g + 1) * n],
+                        start=(g == 0), stop=(g == 1),
+                    )
+                if share_with_vector and lt % 2 == 1:
+                    nc.vector.tensor_scalar_add(out=pbt[:, lt, :], in0=pt[:], scalar1=bias_col[:, lt:lt + 1])
+                else:
+                    nc.scalar.activation(out=pbt[:, lt, :], in_=pt[:], func=ACT.Identity,
+                                         bias=bias_col[:, lt:lt + 1], scale=1.0)
+
+        def b_n_tensor(c):
+            codes, scl = xc[c]
+            for h in range(GRP // 2):
+                pn = psum.tile([P, 2, L], F32, tag="bank")
+                pns[(c, h)] = pn
+                for jj in range(2):
+                    for g in range(2):
+                        c0 = g * n + (2 * h + jj) * P
+                        nc.tensor.matmul_mx(
+                            out=pn[:, jj, :],
+                            lhsT=codes[:, c0:c0 + P].bitcast(FP8X4), lhsT_scale=scl[:, c0:c0 + P],
+                            rhs=wcodes[:, g * G3 + 2 * L:(g + 1) * G3].bitcast(FP8X4),
+                            rhs_scale=wscl[:, g * G3 + 2 * L:(g + 1) * G3],
+                            start=(g == 0), stop=(g == 1),
+                        )
+
+        def b_n_vector(c, h):
+            if h == 0:
+                v = vpl.tile([P, GRP, L], F32)
+                vs[c] = v
+            nc.vector.tensor_tensor(
+                out=vs[c][:, 2 * h:2 * h + 2, :], in0=pns[(c, h)][:],
+                in1=bn_sb[:].unsqueeze(1).to_broadcast([P, 2, L]), op=ALU.add,
+            )
+
+        def c_begin(c):
+            rz = rzp.tile([P, GRP, 2 * L], F32)
+            rzs[c] = rz
+            u = upl.tile([P, GRP, L], F32)
+            us[c] = u
+
+        def c_tile(c, j):
+            acc = psum.tile([P, 2 * L], F32, tag="bank")
+            nc.tensor.matmul(out=acc[:], lhsT=identb[:], rhs=g_sb[c][:, j, 0:2 * L], start=True, stop=False)
+            for lt in range(4):
+                nc.tensor.matmul(
+                    out=acc[:, lt * P:(lt + 1) * P], lhsT=pbts[c][:, lt, j * P:(j + 1) * P], rhs=ident[:],
+                    is_transpose=True, start=False, stop=(lt == 3),
+                )
+            nc.scalar.activation(out=rzs[c][:, j, :], in_=acc[:], func=ACT.Sigmoid)
+
+        def e4(c, h):
+            js = slice(2 * h, 2 * h + 2)
+            nc.vector.tensor_tensor(out=us[c][:, js, :], in0=rzs[c][:, js, 0:L], in1=g_sb[c][:, js, 2 * L:G3], op=ALU.mult)
+
+        def e6(c, h):
+            js = slice(2 * h, 2 * h + 2)
+            nc.vector.tensor_tensor(out=vs[c][:, js, :], in0=vs[c][:, js, :], in1=us[c][:, js, :], op=ALU.add)
+
+        def d_scalar(c, h):
+            js = slice(2 * h, 2 * h + 2)
+            nc.scalar.activation(out=vs[c][:, js, :], in_=vs[c][:, js, :], func=ACT.Tanh)
+
+        def blend_op(c, h, k):
+            if h == 0 and k == 0:
+                o_new = opl.tile([P, GRP, L], F32)
+                outs[c] = o_new
+            js = slice(2 * h, 2 * h + 2)
+            o = outs[c]
+            if k == 0:
+                nc.vector.tensor_tensor(out=o[:, js, :], in0=h_sb[c][:, js, :], in1=vs[c][:, js, :], op=ALU.subtract)
+            elif k == 1:
+                nc.vector.tensor_tensor(out=o[:, js, :], in0=o[:, js, :], in1=rzs[c][:, js, L:2 * L], op=ALU.mult)
+            else:
+                nc.vector.tensor_tensor(out=o[:, js, :], in0=o[:, js, :], in1=vs[c][:, js, :], op=ALU.add)
+                nc.sync.dma_start(out=o_v[:, c * GRP + 2 * h:c * GRP + 2 * h + 2, :], in_=o[:, js, :])
+
+        a_begin(0)
+        for j in range(GRP):
+            a_tile(0, j, j % 2 == 1)
+        a_end(0)
+        prep_w()
+        b_rz(0, True)
+        b_n_tensor(0)
+        b_n_vector(0, 0)
+        b_n_vector(0, 1)
+        a_begin(1)
+        for j in range(GRP):
+            a_tile(1, j, j % 2 == 1)
+        a_end(1)
+        load_x(4, 1)
+        load_gh(2)
+
+        for i in range(NG + 1):
+            if 1 <= i < NG:
+                b_n_vector(i, 0)
+                b_n_vector(i, 1)
+            if i >= 1:
+                for k in range(2):
+                    blend_op(i - 1, 0, k)
+                    blend_op(i - 1, 1, k)
+                blend_op(i - 1, 0, 2)
+            if i < NG:
+                c_begin(i)
+                if i + 2 < NG:
+                    a_begin(i + 2)
+                for j in range(GRP):
+                    c_tile(i, j)
+                    if i + 2 < NG:
+                        a_tile(i + 2, j, False)
+                    if j == 1:
+                        e4(i, 0)
+                        if i >= 1:
+                            blend_op(i - 1, 1, 2)
+                        e6(i, 0)
+                    if j == 3:
+                        e4(i, 1)
+                        if i + 2 < NG:
+                            a_end(i + 2)
+                        e6(i, 1)
+                if i + 5 < NG:
+                    load_x(i + 5, 1)
+                if i + 3 < NG:
+                    load_gh(i + 3)
+            else:
+                blend_op(i - 1, 1, 2)
+            if i + 1 < NG:
+                b_rz(i + 1, False)
+                b_n_tensor(i + 1)
+            if i < NG:
+                for h in range(GRP // 2):
+                    d_scalar(i, h)

@@ -206,15 +206,37 @@ def tile_grucellstack_pa_t_kernel(tc, x, h0, gh0, w_ih0, b_ih0, out):
             u = upl.tile([P, GRP, L], F32)
             us[c] = u
 
-        def c_tile(c, j):
+        def c_tile(c, j, a=None):
             acc = psum.tile([P, 2 * L], F32, tag="bank")
-            nc.tensor.matmul(out=acc[:], lhsT=identb[:], rhs=g_sb[c][:, j, 0:2 * L], start=True, stop=False)
-            for lt in range(4):
+            if a is not None:
+                xt = psum.tile([P, 4, P], F32, tag="bank")
+                words = x_sb[a][:].bitcast(F32)
+
+            def turn_word(q):
+                if a is not None:
+                    w0 = j * (IN // 2) + (q // 2) * 2 * P + q % 2
+                    nc.tensor.transpose(xt[:, q, :], words[:, w0:w0 + 2 * P - 1:2], ident[:])
+
+            def back(lt):
                 nc.tensor.matmul(
                     out=acc[:, lt * P:(lt + 1) * P], lhsT=pbts[c][:, lt, j * P:(j + 1) * P], rhs=ident[:],
                     is_transpose=True, start=False, stop=(lt == 3),
                 )
+
+            for q in range(2):
+                nc.tensor.matmul(out=acc[:, q * L:(q + 1) * L], lhsT=identb[:], rhs=g_sb[c][:, j, q * L:(q + 1) * L],
+                                 start=(q == 0), stop=False)
+                turn_word(q)
+            back(0)
+            turn_word(2)
+            back(1)
+            turn_word(3)
+            back(2)
+            back(3)
             nc.scalar.activation(out=rzs[c][:, j, :], in_=acc[:], func=ACT.Sigmoid)
+            if a is not None:
+                gw = groupeds[a][:].bitcast(F32).rearrange("p (g r u) -> p g r u", g=2, u=2)
+                nc.scalar.copy(out=gw[:, :, j * P:(j + 1) * P, :], in_=xt[:].rearrange("p (g u) r -> p g r u", u=2))
 
         def e4(c, h):
             js = slice(2 * h, 2 * h + 2)
@@ -272,9 +294,7 @@ def tile_grucellstack_pa_t_kernel(tc, x, h0, gh0, w_ih0, b_ih0, out):
                 if i + 2 < NG:
                     a_begin(i + 2)
                 for j in range(GRP):
-                    c_tile(i, j)
-                    if i + 2 < NG:
-                        a_tile(i + 2, j, False)
+                    c_tile(i, j, i + 2 if i + 2 < NG else None)
                     if j == 1:
                         e4(i, 0)
                         if i >= 1:

@@ -81,25 +81,27 @@ def tile_grucellstack_pa_t_kernel(tc, x, h0, gh0, w_ih0, b_ih0, out):
             nc.sync.dma_start(out=ht_in[:], in_=h_v[:, c * GRP:(c + 1) * GRP, :])
             h_sb[c] = ht_in
 
+        load_x(0, 4)
         nc.sync.dma_start(out=brow[0:WT, :], in_=b_ih0.rearrange("(r c) -> r c", c=P))
         nc.sync.dma_start(out=bz[0:1, :], in_=b_ih0.rearrange("(o c) -> o c", o=1)[:, 2 * L:G3])
-        load_x(0, 4)
         for i in range(3):
             nc.sync.dma_start(out=w_sb[:, 2 * i:2 * i + 2, :], in_=w_v[:, 2 * i:2 * i + 2, :])
         load_x(1, 1)
         load_gh(0)
-        load_x(2, 1)
+        load_x(2, 4)
         load_gh(1)
         load_x(3, 1)
 
-        bt_ps = psum.tile([P, P], BF16, tag="bank")
-        nc.tensor.transpose(bt_ps[:], brow[:], identb[:])
         bias_col = const.tile([P, 8], F32)
-        nc.vector.tensor_copy(out=bias_col[:, 0:WT], in_=bt_ps[:, 0:WT])
-        bn_ps = psum.tile([P, L], F32, tag="bank")
-        nc.tensor.matmul(out=bn_ps[:], lhsT=ones[:], rhs=bz[:], start=True, stop=True)
         bn_sb = const.tile([P, L], F32)
-        nc.vector.tensor_copy(out=bn_sb[:], in_=bn_ps[:])
+
+        def bias_setup():
+            bt_ps = psum.tile([P, P], BF16, tag="bank")
+            nc.tensor.transpose(bt_ps[:], brow[:], identb[:])
+            nc.vector.tensor_copy(out=bias_col[:, 0:WT], in_=bt_ps[:, 0:WT])
+            bn_ps = psum.tile([P, L], F32, tag="bank")
+            nc.tensor.matmul(out=bn_ps[:], lhsT=ones[:], rhs=bz[:], start=True, stop=True)
+            nc.vector.tensor_copy(out=bn_sb[:], in_=bn_ps[:])
 
         wcodes = const.tile([P, 2 * G3], U32, align_bytes=64)
         wscl = const.tile([P, 2 * G3], U8, align_bytes=64)
@@ -268,6 +270,7 @@ def tile_grucellstack_pa_t_kernel(tc, x, h0, gh0, w_ih0, b_ih0, out):
         for j in range(GRP):
             a_tile(0, j, j % 2 == 1)
         a_end(0)
+        bias_setup()
         prep_w()
         b_rz(0, True)
         b_n_tensor(0)
@@ -302,9 +305,9 @@ def tile_grucellstack_pa_t_kernel(tc, x, h0, gh0, w_ih0, b_ih0, out):
                         e6(i, 0)
                     if j == 3:
                         e4(i, 1)
+                        e6(i, 1)
                         if i + 2 < NG:
                             a_end(i + 2)
-                        e6(i, 1)
                 if i + 5 < NG:
                     load_x(i + 5, 1)
                 if i + 3 < NG:

@@ -39,8 +39,8 @@ def tile_grucellstack_pa_t_kernel(tc, x, h0, gh0, w_ih0, b_ih0, out):
             ctx.enter_context(tc.manual_schedule())
         const = ctx.enter_context(tc.tile_pool(name="const", bufs=1))
         xin = ctx.enter_context(tc.tile_pool(name="xin", bufs=4))
-        gin = ctx.enter_context(tc.tile_pool(name="gin", bufs=NG))
-        hin = ctx.enter_context(tc.tile_pool(name="hin", bufs=NG))
+        gin = ctx.enter_context(tc.tile_pool(name="gin", bufs=5))
+        hin = ctx.enter_context(tc.tile_pool(name="hin", bufs=5))
         grp = ctx.enter_context(tc.tile_pool(name="grp", bufs=2))
         cod = ctx.enter_context(tc.tile_pool(name="cod", bufs=3))
         pbp = ctx.enter_context(tc.tile_pool(name="pbp", bufs=2))
@@ -86,7 +86,7 @@ def tile_grucellstack_pa_t_kernel(tc, x, h0, gh0, w_ih0, b_ih0, out):
         nc.sync.dma_start(out=bz[0:1, :], in_=b_ih0.rearrange("(o c) -> o c", o=1)[:, 2 * L:G3])
         for i in range(3):
             nc.sync.dma_start(out=w_sb[:, 2 * i:2 * i + 2, :], in_=w_v[:, 2 * i:2 * i + 2, :])
-        load_x(1, 1)
+        load_x(1, 4)
         load_gh(0)
         load_x(2, 4)
         load_gh(1)
@@ -106,18 +106,24 @@ def tile_grucellstack_pa_t_kernel(tc, x, h0, gh0, w_ih0, b_ih0, out):
         wcodes = const.tile([P, 2 * G3], U32, align_bytes=64)
         wscl = const.tile([P, 2 * G3], U8, align_bytes=64)
 
-        def turn(words, col0, dst, on_vector):
+        def turn(words, col0, dst, on_vector, apart=False):
             xt = psum.tile([P, 4, P], F32, tag="bank")
             for q in range(4):
-                w0 = col0 + (q // 2) * 2 * P + q % 2
-                nc.tensor.transpose(xt[:, q, :], words[:, w0:w0 + 2 * P - 1:2], ident[:])
+                if apart:
+                    words_q = words[:, col0 + q * P:col0 + (q + 1) * P]
+                else:
+                    w0 = col0 + (q // 2) * 2 * P + q % 2
+                    words_q = words[:, w0:w0 + 2 * P - 1:2]
+                nc.tensor.transpose(xt[:, q, :], words_q, ident[:])
             src = xt[:].rearrange("p (g u) r -> p g r u", u=2)
             if on_vector:
                 nc.vector.tensor_copy(out=dst, in_=src)
             else:
                 nc.scalar.copy(out=dst, in_=src)
 
+        late = (NG - 1,)
         groupeds = {}
+        apart = {}
         xc = {}
         pbts = {}
         pns = {}
@@ -133,6 +139,22 @@ def tile_grucellstack_pa_t_kernel(tc, x, h0, gh0, w_ih0, b_ih0, out):
         def a_tile(c, j, on_vector):
             gw = groupeds[c][:].bitcast(F32).rearrange("p (g r u) -> p g r u", g=2, u=2)
             turn(x_sb[c][:].bitcast(F32), j * (IN // 2), gw[:, :, j * P:(j + 1) * P, :], on_vector)
+
+        def set_apart(c, j, on_vector):
+            if j == 0:
+                xa = const.tile([P, GRP * IN], BF16)
+                apart[c] = xa
+            words = x_sb[c][:].bitcast(F32)[:, j * (IN // 2):(j + 1) * (IN // 2)]
+            dst = apart[c][:].bitcast(F32)[:, j * (IN // 2):(j + 1) * (IN // 2)].rearrange("p (g u w) -> p g u w", g=2, u=2)
+            src = words.rearrange("p (g w u) -> p g u w", g=2, u=2)
+            if on_vector:
+                nc.vector.tensor_copy(out=dst, in_=src)
+            else:
+                nc.scalar.copy(out=dst, in_=src)
+
+        def a_tile_apart(c, j, on_vector):
+            gw = groupeds[c][:].bitcast(F32).rearrange("p (g r u) -> p g r u", g=2, u=2)
+            turn(apart[c][:].bitcast(F32), j * (IN // 2), gw[:, :, j * P:(j + 1) * P, :], on_vector, True)
 
         def a_end(c):
             codes = cod.tile([P, 2 * n], U32, align_bytes=64)
@@ -157,11 +179,13 @@ def tile_grucellstack_pa_t_kernel(tc, x, h0, gh0, w_ih0, b_ih0, out):
                             in_=wg[:, (2 * k + g) * 4 * P:(2 * k + g + 1) * 4 * P],
                         )
 
-        def b_rz(c, share_with_vector):
+        def b_rz(c, lo, hi):
             codes, scl = xc[c]
-            pbt = pbp.tile([P, 4, n], F32)
-            pbts[c] = pbt
-            for lt in range(4):
+            if lo == 0:
+                pbt = pbp.tile([P, WT if c in late else 4, n], F32)
+                pbts[c] = pbt
+            pbt = pbts[c]
+            for lt in range(lo, hi):
                 pt = psum.tile([P, n], F32, tag="bank")
                 for g in range(2):
                     c0 = g * G3 + lt * P
@@ -171,11 +195,8 @@ def tile_grucellstack_pa_t_kernel(tc, x, h0, gh0, w_ih0, b_ih0, out):
                         rhs=codes[:, g * n:(g + 1) * n].bitcast(FP8X4), rhs_scale=scl[:, g * n:(g + 1) * n],
                         start=(g == 0), stop=(g == 1),
                     )
-                if share_with_vector and lt % 2 == 1:
-                    nc.vector.tensor_scalar_add(out=pbt[:, lt, :], in0=pt[:], scalar1=bias_col[:, lt:lt + 1])
-                else:
-                    nc.scalar.activation(out=pbt[:, lt, :], in_=pt[:], func=ACT.Identity,
-                                         bias=bias_col[:, lt:lt + 1], scale=1.0)
+                nc.scalar.activation(out=pbt[:, lt, :], in_=pt[:], func=ACT.Identity,
+                                     bias=bias_col[:, lt:lt + 1], scale=1.0)
 
         def b_n_tensor(c):
             codes, scl = xc[c]
@@ -193,16 +214,23 @@ def tile_grucellstack_pa_t_kernel(tc, x, h0, gh0, w_ih0, b_ih0, out):
                             start=(g == 0), stop=(g == 1),
                         )
 
+        def n_back(c, h):
+            pn = psum.tile([P, 2, L], F32, tag="bank")
+            pns[(c, h)] = pn
+            for jj in range(2):
+                for k in range(2):
+                    j = 2 * h + jj
+                    nc.tensor.transpose(pn[:, jj, k * P:(k + 1) * P], pbts[c][:, 4 + k, j * P:(j + 1) * P], ident[:])
+
         def b_n_vector(c, h):
-            if h == 0:
-                v = vpl.tile([P, GRP, L], F32)
-                vs[c] = v
             nc.vector.tensor_tensor(
                 out=vs[c][:, 2 * h:2 * h + 2, :], in0=pns[(c, h)][:],
                 in1=bn_sb[:].unsqueeze(1).to_broadcast([P, 2, L]), op=ALU.add,
             )
 
         def c_begin(c):
+            v = vpl.tile([P, GRP, L], F32)
+            vs[c] = v
             rz = rzp.tile([P, GRP, 2 * L], F32)
             rzs[c] = rz
             u = upl.tile([P, GRP, L], F32)
@@ -246,7 +274,8 @@ def tile_grucellstack_pa_t_kernel(tc, x, h0, gh0, w_ih0, b_ih0, out):
 
         def e6(c, h):
             js = slice(2 * h, 2 * h + 2)
-            nc.vector.tensor_tensor(out=vs[c][:, js, :], in0=vs[c][:, js, :], in1=us[c][:, js, :], op=ALU.add)
+            base = pns[(c, h)][:] if c in late else vs[c][:, js, :]
+            nc.vector.tensor_tensor(out=vs[c][:, js, :], in0=base, in1=us[c][:, js, :], op=ALU.add)
 
         def d_scalar(c, h):
             js = slice(2 * h, 2 * h + 2)
@@ -272,32 +301,38 @@ def tile_grucellstack_pa_t_kernel(tc, x, h0, gh0, w_ih0, b_ih0, out):
         a_end(0)
         bias_setup()
         prep_w()
-        b_rz(0, True)
+        for j in range(GRP):
+            set_apart(1, j, True)
+        b_rz(0, 0, 4)
         b_n_tensor(0)
+        c_begin(0)
         b_n_vector(0, 0)
         b_n_vector(0, 1)
         a_begin(1)
         for j in range(GRP):
-            a_tile(1, j, j % 2 == 1)
+            a_tile_apart(1, j, j % 2 == 1)
         a_end(1)
         load_x(4, 1)
         load_gh(2)
 
         for i in range(NG + 1):
             if 1 <= i < NG:
-                b_n_vector(i, 0)
-                b_n_vector(i, 1)
+                c_begin(i)
+                if i not in late:
+                    b_n_vector(i, 0)
+                    b_n_vector(i, 1)
             if i >= 1:
                 for k in range(2):
                     blend_op(i - 1, 0, k)
                     blend_op(i - 1, 1, k)
                 blend_op(i - 1, 0, 2)
             if i < NG:
-                c_begin(i)
                 if i + 2 < NG:
                     a_begin(i + 2)
                 for j in range(GRP):
                     c_tile(i, j, i + 2 if i + 2 < NG else None)
+                    if j % 2 == 1 and i in late:
+                        n_back(i, j // 2)
                     if j == 1:
                         e4(i, 0)
                         if i >= 1:
@@ -305,9 +340,9 @@ def tile_grucellstack_pa_t_kernel(tc, x, h0, gh0, w_ih0, b_ih0, out):
                         e6(i, 0)
                     if j == 3:
                         e4(i, 1)
-                        e6(i, 1)
                         if i + 2 < NG:
                             a_end(i + 2)
+                        e6(i, 1)
                 if i + 5 < NG:
                     load_x(i + 5, 1)
                 if i + 3 < NG:
@@ -315,8 +350,11 @@ def tile_grucellstack_pa_t_kernel(tc, x, h0, gh0, w_ih0, b_ih0, out):
             else:
                 blend_op(i - 1, 1, 2)
             if i + 1 < NG:
-                b_rz(i + 1, False)
-                b_n_tensor(i + 1)
+                b_rz(i + 1, 0, 4)
+                if i + 1 not in late:
+                    b_n_tensor(i + 1)
             if i < NG:
                 for h in range(GRP // 2):
                     d_scalar(i, h)
+            if i + 1 in late:
+                b_rz(i + 1, 4, WT)

@@ -250,19 +250,34 @@ def tile_grucellstack_pa_t_kernel(tc, x, h0, gh0, w_ih0, b_ih0, out):
             def back(lt):
                 nc.tensor.matmul(
                     out=acc[:, lt * P:(lt + 1) * P], lhsT=pbts[c][:, lt, j * P:(j + 1) * P], rhs=ident[:],
-                    is_transpose=True, start=False, stop=(lt == 3),
+                    is_transpose=True, start=False, stop=(lt == 3 and not gh_last),
                 )
 
-            for q in range(2):
+            def keep_gh(q):
                 nc.tensor.matmul(out=acc[:, q * L:(q + 1) * L], lhsT=identb[:], rhs=g_sb[c][:, j, q * L:(q + 1) * L],
-                                 start=(q == 0), stop=False)
-                turn_word(q)
-            back(0)
-            turn_word(2)
-            back(1)
-            turn_word(3)
-            back(2)
-            back(3)
+                                 start=(q == 0), stop=(q == 1 and gh_last))
+
+            gh_last = j == GRP - 1
+            keep_gh(0)
+            turn_word(0)
+            if gh_last:
+                back(0)
+                turn_word(1)
+                back(1)
+                turn_word(2)
+                back(2)
+                turn_word(3)
+                back(3)
+                keep_gh(1)
+            else:
+                keep_gh(1)
+                turn_word(1)
+                back(0)
+                turn_word(2)
+                back(1)
+                turn_word(3)
+                back(2)
+                back(3)
             nc.scalar.activation(out=rzs[c][:, j, :], in_=acc[:], func=ACT.Sigmoid)
             if a is not None:
                 gw = groupeds[a][:].bitcast(F32).rearrange("p (g r u) -> p g r u", g=2, u=2)
@@ -331,15 +346,19 @@ def tile_grucellstack_pa_t_kernel(tc, x, h0, gh0, w_ih0, b_ih0, out):
                     a_begin(i + 2)
                 for j in range(GRP):
                     c_tile(i, j, i + 2 if i + 2 < NG else None)
-                    if j % 2 == 1 and i in late:
-                        n_back(i, j // 2)
                     if j == 1:
                         e4(i, 0)
                         if i >= 1:
                             blend_op(i - 1, 1, 2)
-                        e6(i, 0)
+                        if i not in late:
+                            e6(i, 0)
                     if j == 3:
+                        if i in late:
+                            for h in range(GRP // 2):
+                                n_back(i, h)
                         e4(i, 1)
+                        if i in late:
+                            e6(i, 0)
                         if i + 2 < NG:
                             a_end(i + 2)
                         e6(i, 1)

@@ -103,8 +103,8 @@ def tile_grucellstack_pa_t_kernel(tc, x, h0, gh0, w_ih0, b_ih0, out):
             nc.tensor.matmul(out=bn_ps[:], lhsT=ones[:], rhs=bz[:], start=True, stop=True)
             nc.vector.tensor_copy(out=bn_sb[:], in_=bn_ps[:])
 
-        wcodes = const.tile([P, 2 * G3], U32, align_bytes=64)
-        wscl = const.tile([P, 2 * G3], U8, align_bytes=64)
+        wcodes = const.tile([P, 2 * G3], U32, align_bytes=256)
+        wscl = const.tile([P, 2 * G3], U8, align_bytes=256)
 
         def turn(words, col0, dst, on_vector, apart=False):
             xt = psum.tile([P, 4, P], F32, tag="bank")
@@ -157,8 +157,8 @@ def tile_grucellstack_pa_t_kernel(tc, x, h0, gh0, w_ih0, b_ih0, out):
             turn(apart[c][:].bitcast(F32), j * (IN // 2), gw[:, :, j * P:(j + 1) * P, :], on_vector, True)
 
         def a_end(c):
-            codes = cod.tile([P, 2 * n], U32, align_bytes=64)
-            scl = cod.tile([P, 2 * n], U8, align_bytes=64)
+            codes = cod.tile([P, 2 * n], U32, align_bytes=256)
+            scl = cod.tile([P, 2 * n], U8, align_bytes=256)
             nc.vector.quantize_mx(out=codes[:].bitcast(FP8X4), scales=scl[:], in_=groupeds[c][:])
             xc[c] = (codes, scl)
 
@@ -283,24 +283,27 @@ def tile_grucellstack_pa_t_kernel(tc, x, h0, gh0, w_ih0, b_ih0, out):
                 gw = groupeds[a][:].bitcast(F32).rearrange("p (g r u) -> p g r u", g=2, u=2)
                 nc.scalar.copy(out=gw[:, :, j * P:(j + 1) * P, :], in_=xt[:].rearrange("p (g u) r -> p g r u", u=2))
 
+        def part(h):
+            return h if isinstance(h, slice) else slice(2 * h, 2 * h + 2)
+
         def e4(c, h):
-            js = slice(2 * h, 2 * h + 2)
+            js = part(h)
             nc.vector.tensor_tensor(out=us[c][:, js, :], in0=rzs[c][:, js, 0:L], in1=g_sb[c][:, js, 2 * L:G3], op=ALU.mult)
 
         def e6(c, h):
-            js = slice(2 * h, 2 * h + 2)
-            base = pns[(c, h)][:] if c in late else vs[c][:, js, :]
+            js = part(h)
+            base = pns[(c, js.start // 2)][:, js.start % 2:js.start % 2 + js.stop - js.start, :] if c in late else vs[c][:, js, :]
             nc.vector.tensor_tensor(out=vs[c][:, js, :], in0=base, in1=us[c][:, js, :], op=ALU.add)
 
         def d_scalar(c, h):
-            js = slice(2 * h, 2 * h + 2)
+            js = part(h)
             nc.scalar.activation(out=vs[c][:, js, :], in_=vs[c][:, js, :], func=ACT.Tanh)
 
         def blend_op(c, h, k):
             if h == 0 and k == 0:
                 o_new = opl.tile([P, GRP, L], F32)
                 outs[c] = o_new
-            js = slice(2 * h, 2 * h + 2)
+            js = part(h)
             o = outs[c]
             if k == 0:
                 nc.vector.tensor_tensor(out=o[:, js, :], in0=h_sb[c][:, js, :], in1=vs[c][:, js, :], op=ALU.subtract)
@@ -308,7 +311,7 @@ def tile_grucellstack_pa_t_kernel(tc, x, h0, gh0, w_ih0, b_ih0, out):
                 nc.vector.tensor_tensor(out=o[:, js, :], in0=o[:, js, :], in1=rzs[c][:, js, L:2 * L], op=ALU.mult)
             else:
                 nc.vector.tensor_tensor(out=o[:, js, :], in0=o[:, js, :], in1=vs[c][:, js, :], op=ALU.add)
-                nc.sync.dma_start(out=o_v[:, c * GRP + 2 * h:c * GRP + 2 * h + 2, :], in_=o[:, js, :])
+                nc.sync.dma_start(out=o_v[:, c * GRP + js.start:c * GRP + js.stop, :], in_=o[:, js, :])
 
         a_begin(0)
         for j in range(GRP):
@@ -330,13 +333,14 @@ def tile_grucellstack_pa_t_kernel(tc, x, h0, gh0, w_ih0, b_ih0, out):
         load_x(4, 1)
         load_gh(2)
 
+        last2, last3 = slice(2, 3), slice(3, 4)
         for i in range(NG + 1):
             if 1 <= i < NG:
                 c_begin(i)
                 if i not in late:
                     b_n_vector(i, 0)
                     b_n_vector(i, 1)
-            if i >= 1:
+            if 1 <= i < NG:
                 for k in range(2):
                     blend_op(i - 1, 0, k)
                     blend_op(i - 1, 1, k)
@@ -356,24 +360,31 @@ def tile_grucellstack_pa_t_kernel(tc, x, h0, gh0, w_ih0, b_ih0, out):
                         if i in late:
                             for h in range(GRP // 2):
                                 n_back(i, h)
-                        e4(i, 1)
                         if i in late:
+                            e4(i, last2)
                             e6(i, 0)
+                            e4(i, last3)
+                            e6(i, last2)
+                            e6(i, last3)
+                        else:
+                            e4(i, 1)
                         if i + 2 < NG:
                             a_end(i + 2)
-                        e6(i, 1)
+                        if i not in late:
+                            e6(i, 1)
                 if i + 5 < NG:
                     load_x(i + 5, 1)
                 if i + 3 < NG:
                     load_gh(i + 3)
             else:
-                blend_op(i - 1, 1, 2)
+                for js, k in ((0, 0), (0, 1), (last2, 0), (0, 2), (last3, 0), (last2, 1), (last3, 1), (last2, 2), (last3, 2)):
+                    blend_op(i - 1, js, k)
             if i + 1 < NG:
                 b_rz(i + 1, 0, 4)
                 if i + 1 not in late:
                     b_n_tensor(i + 1)
             if i < NG:
-                for h in range(GRP // 2):
+                for h in (0, last2, last3) if i in late else (0, 1):
                     d_scalar(i, h)
             if i + 1 in late:
                 b_rz(i + 1, 4, WT)

@@ -44,6 +44,7 @@ def tile_grucellstack_pa_t_kernel(tc, x, h0, gh0, w_ih0, b_ih0, out):
         grp = ctx.enter_context(tc.tile_pool(name="grp", bufs=2))
         cod = ctx.enter_context(tc.tile_pool(name="cod", bufs=3))
         pbp = ctx.enter_context(tc.tile_pool(name="pbp", bufs=2))
+        hap = ctx.enter_context(tc.tile_pool(name="hap", bufs=2))
         rzp = ctx.enter_context(tc.tile_pool(name="rzp", bufs=3))
         vpl = ctx.enter_context(tc.tile_pool(name="vpl", bufs=4))
         upl = ctx.enter_context(tc.tile_pool(name="upl", bufs=2))
@@ -236,6 +237,14 @@ def tile_grucellstack_pa_t_kernel(tc, x, h0, gh0, w_ih0, b_ih0, out):
             u = upl.tile([P, GRP, L], F32)
             us[c] = u
 
+        half_apart = {}
+
+        def set_half_apart(c, j):
+            ha = hap.tile([P, IN // 2], BF16)
+            half_apart[(c, j)] = ha
+            words = x_sb[c][:].bitcast(F32)[:, j * (IN // 2) + 2 * P:(j + 1) * (IN // 2)]
+            nc.vector.tensor_copy(out=ha[:].bitcast(F32).rearrange("p (u w) -> p u w", u=2), in_=words.rearrange("p (w u) -> p u w", u=2))
+
         def c_tile(c, j, a=None):
             acc = psum.tile([P, 2 * L], F32, tag="bank")
             if a is not None:
@@ -243,7 +252,10 @@ def tile_grucellstack_pa_t_kernel(tc, x, h0, gh0, w_ih0, b_ih0, out):
                 words = x_sb[a][:].bitcast(F32)
 
             def turn_word(q):
-                if a is not None:
+                if a is not None and q >= 2 and (a, j) in half_apart:
+                    hw = half_apart[(a, j)][:].bitcast(F32)
+                    nc.tensor.transpose(xt[:, q, :], hw[:, (q - 2) * P:(q - 1) * P], ident[:])
+                elif a is not None:
                     w0 = j * (IN // 2) + (q // 2) * 2 * P + q % 2
                     nc.tensor.transpose(xt[:, q, :], words[:, w0:w0 + 2 * P - 1:2], ident[:])
 
@@ -279,6 +291,8 @@ def tile_grucellstack_pa_t_kernel(tc, x, h0, gh0, w_ih0, b_ih0, out):
                 back(2)
                 back(3)
             nc.scalar.activation(out=rzs[c][:, j, :], in_=acc[:], func=ACT.Sigmoid)
+            if c == NG - 1 and j >= 2:
+                nc.scalar.activation(out=keep[:, j - 2, :], in_=acc[:, L:2 * L], func=ACT.Sigmoid, scale=-1.0)
             if a is not None:
                 gw = groupeds[a][:].bitcast(F32).rearrange("p (g r u) -> p g r u", g=2, u=2)
                 nc.scalar.copy(out=gw[:, :, j * P:(j + 1) * P, :], in_=xt[:].rearrange("p (g u) r -> p g r u", u=2))
@@ -334,6 +348,18 @@ def tile_grucellstack_pa_t_kernel(tc, x, h0, gh0, w_ih0, b_ih0, out):
         load_gh(2)
 
         last2, last3 = slice(2, 3), slice(3, 4)
+        keep = const.tile([P, 2, L], F32)
+        zh = const.tile([P, 2, L], F32)
+
+        def new_part(js, k):
+            c = NG - 1
+            q = slice(js.start - 2, js.stop - 2)
+            if k == 0:
+                nc.vector.tensor_tensor(out=keep[:, q, :], in0=keep[:, q, :], in1=vs[c][:, js, :], op=ALU.mult)
+            else:
+                nc.vector.tensor_tensor(out=outs[c][:, js, :], in0=keep[:, q, :], in1=zh[:, q, :], op=ALU.add)
+                nc.sync.dma_start(out=o_v[:, c * GRP + js.start:c * GRP + js.stop, :], in_=outs[c][:, js, :])
+
         for i in range(NG + 1):
             if 1 <= i < NG:
                 c_begin(i)
@@ -348,6 +374,9 @@ def tile_grucellstack_pa_t_kernel(tc, x, h0, gh0, w_ih0, b_ih0, out):
             if i < NG:
                 if i + 2 < NG:
                     a_begin(i + 2)
+                if i == 0:
+                    for j in (2, 3):
+                        set_half_apart(i + 2, j)
                 for j in range(GRP):
                     c_tile(i, j, i + 2 if i + 2 < NG else None)
                     if j == 1:
@@ -377,8 +406,14 @@ def tile_grucellstack_pa_t_kernel(tc, x, h0, gh0, w_ih0, b_ih0, out):
                 if i + 3 < NG:
                     load_gh(i + 3)
             else:
-                for js, k in ((0, 0), (0, 1), (last2, 0), (0, 2), (last3, 0), (last2, 1), (last3, 1), (last2, 2), (last3, 2)):
-                    blend_op(i - 1, js, k)
+                nc.vector.tensor_tensor(out=zh[:], in0=rzs[i - 1][:, 2:4, L:2 * L], in1=h_sb[i - 1][:, 2:4, :], op=ALU.mult)
+                blend_op(i - 1, 0, 0)
+                blend_op(i - 1, 0, 1)
+                new_part(last2, 0)
+                blend_op(i - 1, 0, 2)
+                new_part(last3, 0)
+                new_part(last2, 1)
+                new_part(last3, 1)
             if i + 1 < NG:
                 b_rz(i + 1, 0, 4)
                 if i + 1 not in late:

@@ -169,7 +169,7 @@ def tile_grucellstack_pa_t_kernel(tc, x, h0, gh0, w_ih0, b_ih0, out):
                 for k in range(2):
                     lt = 2 * half + k
                     dst = wg[:, k * 8 * P:(k + 1) * 8 * P].bitcast(F32).rearrange("p (g r u) -> p g r u", g=2, u=2)
-                    turn(w_sb[:, lt, :].bitcast(F32), 0, dst, k == 1)
+                    turn(w_sb[:, lt, :].bitcast(F32), 0, dst, False)
                 for k in range(2):
                     lt = 2 * half + k
                     for g in range(2):
@@ -243,7 +243,8 @@ def tile_grucellstack_pa_t_kernel(tc, x, h0, gh0, w_ih0, b_ih0, out):
             ha = hap.tile([P, IN // 2], BF16)
             half_apart[(c, j)] = ha
             words = x_sb[c][:].bitcast(F32)[:, j * (IN // 2) + 2 * P:(j + 1) * (IN // 2)]
-            nc.vector.tensor_copy(out=ha[:].bitcast(F32).rearrange("p (u w) -> p u w", u=2), in_=words.rearrange("p (w u) -> p u w", u=2))
+            move = nc.vector.tensor_copy if c == 2 else nc.scalar.copy
+            move(out=ha[:].bitcast(F32).rearrange("p (u w) -> p u w", u=2), in_=words.rearrange("p (w u) -> p u w", u=2))
 
         def c_tile(c, j, a=None):
             acc = psum.tile([P, 2 * L], F32, tag="bank")
@@ -374,8 +375,8 @@ def tile_grucellstack_pa_t_kernel(tc, x, h0, gh0, w_ih0, b_ih0, out):
             if i < NG:
                 if i + 2 < NG:
                     a_begin(i + 2)
-                if i == 0:
-                    for j in (2, 3):
+                if i < 2:
+                    for j in (2, 3) if i == 0 else (3,):
                         set_half_apart(i + 2, j)
                 for j in range(GRP):
                     c_tile(i, j, i + 2 if i + 2 < NG else None)

from contextlib import ExitStack

import concourse.mybir as mybir
from concourse.masks import make_identity

F32 = mybir.dt.float32
BF16 = mybir.dt.bfloat16
U32 = mybir.dt.uint32
U8 = mybir.dt.uint8
FP8X4 = mybir.dt.float8_e4m3fn_x4
ACT = mybir.ActivationFunctionType
ALU = mybir.AluOpType

P = 128
B = 4096
IN = 1024
L = 256
G3 = 3 * L
NT = B // P
GRP = 4
NG = NT // GRP
WT = G3 // P
PIN = True

FLOPS = 2 * B * IN * G3


def tile_grucellstack_pa_t_kernel(tc, x, h0, gh0, w_ih0, b_ih0, out):
    nc = tc.nc
    x_v = x.rearrange("(p t) k -> p (t k)", t=NT)
    g_v = gh0.rearrange("(p t) c -> p t c", t=NT)
    h_v = h0.rearrange("(p t) c -> p t c", t=NT)
    o_v = out.rearrange("(p t) c -> p t c", t=NT)
    w_v = w_ih0.rearrange("(t p) k -> p t k", p=P)
    n = GRP * P

    with ExitStack() as ctx:
        if PIN:
            ctx.enter_context(tc.manual_schedule())
        const = ctx.enter_context(tc.tile_pool(name="const", bufs=1))
        xin = ctx.enter_context(tc.tile_pool(name="xin", bufs=4))
        gin = ctx.enter_context(tc.tile_pool(name="gin", bufs=5))
        hin = ctx.enter_context(tc.tile_pool(name="hin", bufs=5))
        grp = ctx.enter_context(tc.tile_pool(name="grp", bufs=2))
        cod = ctx.enter_context(tc.tile_pool(name="cod", bufs=3))
        pbp = ctx.enter_context(tc.tile_pool(name="pbp", bufs=2))
        hap = ctx.enter_context(tc.tile_pool(name="hap", bufs=2))
        rzp = ctx.enter_context(tc.tile_pool(name="rzp", bufs=3))
        vpl = ctx.enter_context(tc.tile_pool(name="vpl", bufs=4))
        upl = ctx.enter_context(tc.tile_pool(name="upl", bufs=2))
        opl = ctx.enter_context(tc.tile_pool(name="opl", bufs=3))
        psum = ctx.enter_context(tc.psum_pool(name="psum", bufs=8))

        brow = const.tile([P, P], BF16)
        nc.vector.memset(brow[:], 0.0)
        bz = const.tile([P, L], BF16)
        nc.vector.memset(bz[:], 0.0)
        ones = const.tile([P, P], BF16)
        nc.vector.memset(ones[:], 1.0)
        ident = const.tile([P, P], F32)
        make_identity(nc, ident[:])
        identb = const.tile([P, P], BF16)
        make_identity(nc, identb[:])

        x_sb = {}
        g_sb = {}
        h_sb = {}
        w_sb = const.tile([P, WT, IN], BF16)

        def load_x(c, pieces):
            xt_in = xin.tile([P, GRP * IN], BF16)
            w = GRP * IN // pieces
            for k in range(pieces):
                nc.sync.dma_start(out=xt_in[:, k * w:(k + 1) * w], in_=x_v[:, c * GRP * IN + k * w:c * GRP * IN + (k + 1) * w])
            x_sb[c] = xt_in

        def load_gh(c):
            gt_in = gin.tile([P, GRP, G3], BF16)
            nc.sync.dma_start(out=gt_in[:], in_=g_v[:, c * GRP:(c + 1) * GRP, :])
            g_sb[c] = gt_in
            ht_in = hin.tile([P, GRP, L], BF16)
            nc.sync.dma_start(out=ht_in[:], in_=h_v[:, c * GRP:(c + 1) * GRP, :])
            h_sb[c] = ht_in

        load_x(0, 4)
        nc.sync.dma_start(out=brow[0:WT, :], in_=b_ih0.rearrange("(r c) -> r c", c=P))
        nc.sync.dma_start(out=bz[0:1, :], in_=b_ih0.rearrange("(o c) -> o c", o=1)[:, 2 * L:G3])
        for i in range(3):
            nc.sync.dma_start(out=w_sb[:, 2 * i:2 * i + 2, :], in_=w_v[:, 2 * i:2 * i + 2, :])
        load_x(1, 4)
        load_gh(0)
        load_x(2, 4)
        load_gh(1)
        load_x(3, 1)

        bias_col = const.tile([P, 8], F32)
        bn_sb = const.tile([P, L], F32)

        def bias_setup():
            bt_ps = psum.tile([P, P], BF16, tag="bank")
            nc.tensor.transpose(bt_ps[:], brow[:], identb[:])
            nc.vector.tensor_copy(out=bias_col[:, 0:WT], in_=bt_ps[:, 0:WT])
            bn_ps = psum.tile([P, L], F32, tag="bank")
            nc.tensor.matmul(out=bn_ps[:], lhsT=ones[:], rhs=bz[:], start=True, stop=True)
            nc.vector.tensor_copy(out=bn_sb[:], in_=bn_ps[:])

        wcodes = const.tile([P, 2 * G3], U32, align_bytes=256)
        wscl = const.tile([P, 2 * G3], U8, align_bytes=256)

        def turn(words, col0, dst, on_vector, apart=False):
            xt = psum.tile([P, 4, P], F32, tag="bank")
            for q in range(4):
                if apart:
                    words_q = words[:, col0 + q * P:col0 + (q + 1) * P]
                else:
                    w0 = col0 + (q // 2) * 2 * P + q % 2
                    words_q = words[:, w0:w0 + 2 * P - 1:2]
                nc.tensor.transpose(xt[:, q, :], words_q, ident[:])
            src = xt[:].rearrange("p (g u) r -> p g r u", u=2)
            if on_vector:
                nc.vector.tensor_copy(out=dst, in_=src)
            else:
                nc.scalar.copy(out=dst, in_=src)

        late = (NG - 1,)
        groupeds = {}
        apart = {}
        xc = {}
        pbts = {}
        pns = {}
        vs = {}
        us = {}
        rzs = {}
        outs = {}

        def a_begin(c):
            grouped = grp.tile([P, 8 * n], BF16, align_bytes=64)
            groupeds[c] = grouped

        def a_tile(c, j, on_vector):
            gw = groupeds[c][:].bitcast(F32).rearrange("p (g r u) -> p g r u", g=2, u=2)
            turn(x_sb[c][:].bitcast(F32), j * (IN // 2), gw[:, :, j * P:(j + 1) * P, :], on_vector)

        def set_apart(c, j, on_vector):
            if j == 0:
                xa = const.tile([P, GRP * IN], BF16)
                apart[c] = xa
            words = x_sb[c][:].bitcast(F32)[:, j * (IN // 2):(j + 1) * (IN // 2)]
            dst = apart[c][:].bitcast(F32)[:, j * (IN // 2):(j + 1) * (IN // 2)].rearrange("p (g u w) -> p g u w", g=2, u=2)
            src = words.rearrange("p (g w u) -> p g u w", g=2, u=2)
            if on_vector:
                nc.vector.tensor_copy(out=dst, in_=src)
            else:
                nc.scalar.copy(out=dst, in_=src)

        def a_tile_apart(c, j, on_vector):
            gw = groupeds[c][:].bitcast(F32).rearrange("p (g r u) -> p g r u", g=2, u=2)
            turn(apart[c][:].bitcast(F32), j * (IN // 2), gw[:, :, j * P:(j + 1) * P, :], on_vector, True)

        def a_end(c):
            codes = cod.tile([P, 2 * n], U32, align_bytes=256)
            scl = cod.tile([P, 2 * n], U8, align_bytes=256)
            nc.vector.quantize_mx(out=codes[:].bitcast(FP8X4), scales=scl[:], in_=groupeds[c][:])
            xc[c] = (codes, scl)

        def prep_w():
            for half in range(3):
                wg = grp.tile([P, 8 * n], BF16, align_bytes=64, tag="grouped")
                for k in range(2):
                    lt = 2 * half + k
                    dst = wg[:, k * 8 * P:(k + 1) * 8 * P].bitcast(F32).rearrange("p (g r u) -> p g r u", g=2, u=2)
                    turn(w_sb[:, lt, :].bitcast(F32), 0, dst, False)
                for k in range(2):
                    lt = 2 * half + k
                    for g in range(2):
                        c0 = g * G3 + lt * P
                        nc.vector.quantize_mx(
                            out=wcodes[:, c0:c0 + P].bitcast(FP8X4),
                            scales=wscl[:, c0:c0 + P],
                            in_=wg[:, (2 * k + g) * 4 * P:(2 * k + g + 1) * 4 * P],
                        )

        def b_rz(c, lo, hi):
            codes, scl = xc[c]
            if lo == 0:
                pbt = pbp.tile([P, WT if c in late else 4, n], F32)
                pbts[c] = pbt
            pbt = pbts[c]
            for lt in range(lo, hi):
                pt = psum.tile([P, n], F32, tag="bank")
                for g in range(2):
                    c0 = g * G3 + lt * P
                    nc.tensor.matmul_mx(
                        out=pt[:],
                        lhsT=wcodes[:, c0:c0 + P].bitcast(FP8X4), lhsT_scale=wscl[:, c0:c0 + P],
                        rhs=codes[:, g * n:(g + 1) * n].bitcast(FP8X4), rhs_scale=scl[:, g * n:(g + 1) * n],
                        start=(g == 0), stop=(g == 1),
                    )
                nc.scalar.activation(out=pbt[:, lt, :], in_=pt[:], func=ACT.Identity,
                                     bias=bias_col[:, lt:lt + 1], scale=1.0)

        def b_n_tensor(c):
            codes, scl = xc[c]
            for h in range(GRP // 2):
                pn = psum.tile([P, 2, L], F32, tag="bank")
                pns[(c, h)] = pn
                for jj in range(2):
                    for g in range(2):
                        c0 = g * n + (2 * h + jj) * P
                        nc.tensor.matmul_mx(
                            out=pn[:, jj, :],
                            lhsT=codes[:, c0:c0 + P].bitcast(FP8X4), lhsT_scale=scl[:, c0:c0 + P],
                            rhs=wcodes[:, g * G3 + 2 * L:(g + 1) * G3].bitcast(FP8X4),
                            rhs_scale=wscl[:, g * G3 + 2 * L:(g + 1) * G3],
                            start=(g == 0), stop=(g == 1),
                        )

        def n_back(c, h):
            pn = psum.tile([P, 2, L], F32, tag="bank")
            pns[(c, h)] = pn
            for jj in range(2):
                for k in range(2):
                    j = 2 * h + jj
                    nc.tensor.transpose(pn[:, jj, k * P:(k + 1) * P], pbts[c][:, 4 + k, j * P:(j + 1) * P], ident[:])

        def b_n_vector(c, h):
            nc.vector.tensor_tensor(
                out=vs[c][:, 2 * h:2 * h + 2, :], in0=pns[(c, h)][:],
                in1=bn_sb[:].unsqueeze(1).to_broadcast([P, 2, L]), op=ALU.add,
            )

        def c_begin(c):
            v = vpl.tile([P, GRP, L], F32)
            vs[c] = v
            rz = rzp.tile([P, GRP, 2 * L], F32)
            rzs[c] = rz
            u = upl.tile([P, GRP, L], F32)
            us[c] = u

        half_apart = {}

        def set_half_apart(c, j):
            ha = hap.tile([P, IN // 2], BF16)
            half_apart[(c, j)] = ha
            words = x_sb[c][:].bitcast(F32)[:, j * (IN // 2) + 2 * P:(j + 1) * (IN // 2)]
            move = nc.vector.tensor_copy if c == 2 else nc.scalar.copy
            move(out=ha[:].bitcast(F32).rearrange("p (u w) -> p u w", u=2), in_=words.rearrange("p (w u) -> p u w", u=2))

        def c_tile(c, j, a=None):
            acc = psum.tile([P, 2 * L], F32, tag="bank")
            if a is not None:
                xt = psum.tile([P, 4, P], F32, tag="bank")
                words = x_sb[a][:].bitcast(F32)

            def turn_word(q):
                if a is not None and q >= 2 and (a, j) in half_apart:
                    hw = half_apart[(a, j)][:].bitcast(F32)
                    nc.tensor.transpose(xt[:, q, :], hw[:, (q - 2) * P:(q - 1) * P], ident[:])
                elif a is not None:
                    w0 = j * (IN // 2) + (q // 2) * 2 * P + q % 2
                    nc.tensor.transpose(xt[:, q, :], words[:, w0:w0 + 2 * P - 1:2], ident[:])

            def back(lt):
                nc.tensor.matmul(
                    out=acc[:, lt * P:(lt + 1) * P], lhsT=pbts[c][:, lt, j * P:(j + 1) * P], rhs=ident[:],
                    is_transpose=True, start=False, stop=(lt == 3 and not gh_last),
                )

            def keep_gh(q):
                nc.tensor.matmul(out=acc[:, q * L:(q + 1) * L], lhsT=identb[:], rhs=g_sb[c][:, j, q * L:(q + 1) * L],
                                 start=(q == 0), stop=(q == 1 and gh_last))

            gh_last = j == GRP - 1
            keep_gh(0)
            turn_word(0)
            if gh_last:
                back(0)
                turn_word(1)
                back(1)
                turn_word(2)
                back(2)
                turn_word(3)
                back(3)
                keep_gh(1)
            else:
                keep_gh(1)
                turn_word(1)
                back(0)
                turn_word(2)
                back(1)
                turn_word(3)
                back(2)
                back(3)
            nc.scalar.activation(out=rzs[c][:, j, :], in_=acc[:], func=ACT.Sigmoid)
            if c == NG - 1 and j >= 2:
                nc.scalar.activation(out=keep[:, j - 2, :], in_=acc[:, L:2 * L], func=ACT.Sigmoid, scale=-1.0)
            if a is not None:
                gw = groupeds[a][:].bitcast(F32).rearrange("p (g r u) -> p g r u", g=2, u=2)
                nc.scalar.copy(out=gw[:, :, j * P:(j + 1) * P, :], in_=xt[:].rearrange("p (g u) r -> p g r u", u=2))

        def part(h):
            return h if isinstance(h, slice) else slice(2 * h, 2 * h + 2)

        def e4(c, h):
            js = part(h)
            nc.vector.tensor_tensor(out=us[c][:, js, :], in0=rzs[c][:, js, 0:L], in1=g_sb[c][:, js, 2 * L:G3], op=ALU.mult)

        def e6(c, h):
            js = part(h)
            base = pns[(c, js.start // 2)][:, js.start % 2:js.start % 2 + js.stop - js.start, :] if c in late else vs[c][:, js, :]
            nc.vector.tensor_tensor(out=vs[c][:, js, :], in0=base, in1=us[c][:, js, :], op=ALU.add)

        def d_scalar(c, h):
            js = part(h)
            nc.scalar.activation(out=vs[c][:, js, :], in_=vs[c][:, js, :], func=ACT.Tanh)

        def blend_op(c, h, k):
            if h == 0 and k == 0:
                o_new = opl.tile([P, GRP, L], F32)
                outs[c] = o_new
            js = part(h)
            o = outs[c]
            if k == 0:
                nc.vector.tensor_tensor(out=o[:, js, :], in0=h_sb[c][:, js, :], in1=vs[c][:, js, :], op=ALU.subtract)
            elif k == 1:
                nc.vector.tensor_tensor(out=o[:, js, :], in0=o[:, js, :], in1=rzs[c][:, js, L:2 * L], op=ALU.mult)
            else:
                nc.vector.tensor_tensor(out=o[:, js, :], in0=o[:, js, :], in1=vs[c][:, js, :], op=ALU.add)
                nc.sync.dma_start(out=o_v[:, c * GRP + js.start:c * GRP + js.stop, :], in_=o[:, js, :])

        a_begin(0)
        for j in range(GRP):
            a_tile(0, j, j % 2 == 1)
        a_end(0)
        bias_setup()
        prep_w()
        for j in range(GRP):
            set_apart(1, j, True)
        b_rz(0, 0, 4)
        b_n_tensor(0)
        c_begin(0)
        b_n_vector(0, 0)
        b_n_vector(0, 1)
        a_begin(1)
        for j in range(GRP):
            a_tile_apart(1, j, j % 2 == 1)
        a_end(1)
        load_x(4, 1)
        load_gh(2)

        last2, last3 = slice(2, 3), slice(3, 4)
        keep = const.tile([P, 2, L], F32)
        zh = const.tile([P, 2, L], F32)

        def new_part(js, k):
            c = NG - 1
            q = slice(js.start - 2, js.stop - 2)
            if k == 0:
                nc.vector.tensor_tensor(out=keep[:, q, :], in0=keep[:, q, :], in1=vs[c][:, js, :], op=ALU.mult)
            else:
                nc.vector.tensor_tensor(out=outs[c][:, js, :], in0=keep[:, q, :], in1=zh[:, q, :], op=ALU.add)
                nc.sync.dma_start(out=o_v[:, c * GRP + js.start:c * GRP + js.stop, :], in_=outs[c][:, js, :])

        for i in range(NG + 1):
            if 1 <= i < NG:
                c_begin(i)
                if i not in late:
                    b_n_vector(i, 0)
                    b_n_vector(i, 1)
            if 1 <= i < NG:
                for k in range(2):
                    blend_op(i - 1, 0, k)
                    blend_op(i - 1, 1, k)
                blend_op(i - 1, 0, 2)
            if i < NG:
                if i + 2 < NG:
                    a_begin(i + 2)
                if i < 2:
                    for j in (2, 3) if i == 0 else (3,):
                        set_half_apart(i + 2, j)
                for j in range(GRP):
                    c_tile(i, j, i + 2 if i + 2 < NG else None)
                    if j == 1:
                        e4(i, 0)
                        if i >= 1:
                            blend_op(i - 1, 1, 2)
                        if i not in late:
                            e6(i, 0)
                    if j == 3:
                        if i in late:
                            for h in range(GRP // 2):
                                n_back(i, h)
                        if i in late:
                            e4(i, last2)
                            e6(i, 0)
                            e4(i, last3)
                            e6(i, last2)
                            e6(i, last3)
                        else:
                            e4(i, 1)
                        if i + 2 < NG:
                            a_end(i + 2)
                        if i not in late:
                            e6(i, 1)
                if i + 5 < NG:
                    load_x(i + 5, 1)
                if i + 3 < NG:
                    load_gh(i + 3)
            else:
                nc.vector.tensor_tensor(out=zh[:], in0=rzs[i - 1][:, 2:4, L:2 * L], in1=h_sb[i - 1][:, 2:4, :], op=ALU.mult)
                blend_op(i - 1, 0, 0)
                blend_op(i - 1, 0, 1)
                new_part(last2, 0)
                blend_op(i - 1, 0, 2)
                new_part(last3, 0)
                new_part(last2, 1)
                new_part(last3, 1)
            if i + 1 < NG:
                b_rz(i + 1, 0, 4)
                if i + 1 not in late:
                    b_n_tensor(i + 1)
            if i < NG:
                for h in (0, last2, last3) if i in late else (0, 1):
                    d_scalar(i, h)
            if i + 1 in late:
                b_rz(i + 1, 4, WT)
